import numpy as np
import ml_dtypes


def mxq(x, axis, fmt="e4m3"):
    dtype, down = {"e4m3": (ml_dtypes.float8_e4m3fn, 7), "e5m2": (ml_dtypes.float8_e5m2, 14)}[fmt]
    v = np.moveaxis(np.asarray(x, np.float32).astype(ml_dtypes.bfloat16).astype(np.float64), axis, -1)
    blocks = v.reshape(v.shape[:-1] + (-1, 32))
    amax = np.abs(blocks).max(-1, keepdims=True)
    byte = np.maximum(np.where(amax > 0, np.frexp(amax)[1] - 1 + 127, 0) - down, 1)
    scale = np.exp2(byte - 127.0)
    codes = (blocks / scale).astype(np.float32).astype(dtype).astype(np.float64)
    return np.moveaxis((codes * scale).reshape(v.shape), -1, axis)


WIDE = False


def mx_kscale(k):
    if not WIDE:
        return np.ones(k)
    levels = np.array([10, -10, 5, -5, 0])
    if k % 512:
        return np.exp2(np.random.permutation(np.resize(levels, k // 32))).repeat(32)
    a = np.empty((k // 512, 16))
    for p in range(k // 512):
        a[p, :8] = np.random.permutation(np.resize(levels, 8))
        for g in range(8):
            far = levels[np.abs(levels - a[p, g]) >= 10]
            a[p, g + 8] = far[np.random.randint(len(far))]
    return np.exp2(a.ravel()).repeat(32)


BF16 = ml_dtypes.bfloat16


def bf(x):
    return np.asarray(x, np.float32).astype(BF16)


def f64(x):
    return np.asarray(x).astype(np.float64)


S, HID, NH, Q_LORA, KV_LORA, NOPE, ROPE, VDIM, BLK = 512, 2048, 16, 1536, 512, 128, 64, 128, 128
EPS = 1e-6


def blockscale(rows, cols, k, g):
    return bf((np.random.random((rows, cols)) * 0.8 + 0.2) * g / np.sqrt(k))


def dequant(w, s):
    so = np.repeat(s, BLK, axis=0)[: w.shape[0]]
    se = np.repeat(so, BLK, axis=1)[:, : w.shape[1]]
    return w * se


def rmsnorm(x, w):
    var = np.mean(x * x, axis=-1, keepdims=True)
    return x * (1.0 / np.sqrt(var + EPS)) * w


def setup_inputs():
    s, t = mx_kscale(HID), mx_kscale(KV_LORA)
    return {"hidden_states": bf(np.random.standard_normal((S, HID)) * s),
            "wkv_a_lat": bf(np.random.standard_normal((KV_LORA, HID)) / s[None, :]),
            "skv_a_lat": blockscale(KV_LORA // BLK, HID // BLK, HID, 1.0),
            "wkv_b": bf(np.random.standard_normal((NH * (NOPE + VDIM), KV_LORA)) / t[None, :]),
            "skv_b": blockscale(NH * (NOPE + VDIM) // BLK, KV_LORA // BLK, KV_LORA, 2.0),
            "kv_ln_w": bf((1.0 + 0.1 * np.random.standard_normal(KV_LORA)) * t)}


def reference(hidden_states, wkv_a_lat, skv_a_lat, wkv_b, skv_b, kv_ln_w):
    wa = dequant(f64(wkv_a_lat), f64(skv_a_lat))
    lkv = mxq(f64(hidden_states), 1, "e4m3") @ mxq(wa, 1, "e4m3").T
    kv_nope = rmsnorm(lkv, f64(kv_ln_w))
    wb = dequant(f64(wkv_b), f64(skv_b))
    kvb = (mxq(kv_nope, 1, "e4m3") @ mxq(wb, 1, "e4m3").T).reshape(S, NH, NOPE + VDIM)
    return kvb[..., :NOPE], kvb[..., NOPE:]

from contextlib import ExitStack

import concourse.mybir as mybir
from concourse.masks import make_identity

F32 = mybir.dt.float32
BF16 = mybir.dt.bfloat16
U32 = mybir.dt.uint32
U8 = mybir.dt.uint8
FP8X4 = mybir.dt.float8_e4m3fn_x4
ACT = mybir.ActivationFunctionType
ALU = mybir.AluOpType

P = 128
QUADRANT = P // 4
TOKENS = 512
HIDDEN = 2048
LATENT = 512
HEADS = 16
HEAD_DIM = 128
KINDS = 2
EPS = 1e-6

PACK = 4
K_PASS = P * PACK
PASSES_A = HIDDEN // K_PASS
TOKEN_TILES = TOKENS // P
LATENT_TILES = LATENT // P
BANK = 512
PSUM_BANKS = 8
HEADS_PER_CHUNK = BANK // HEAD_DIM
CHUNKS_PER_KIND = HEADS // HEADS_PER_CHUNK
CHUNKS = KINDS * CHUNKS_PER_KIND
FACTORS_A = (LATENT // P) * (HIDDEN // P)
FACTORS_B = (HEADS * KINDS) * (LATENT // P)

FLOPS = 2 * TOKENS * LATENT * HIDDEN + 2 * TOKENS * HEADS * KINDS * HEAD_DIM * LATENT


def tile_deepseekv3attention_pb_kernel(
    tc, hidden_states, wkv_a_lat, skv_a_lat, wkv_b, skv_b, kv_ln_w, out_0, out_1
):
    nc = tc.nc
    with ExitStack() as stack:
        const = stack.enter_context(tc.tile_pool(name="const", bufs=1))
        loaded = stack.enter_context(tc.tile_pool(name="loaded", bufs=1))
        quantised = stack.enter_context(tc.tile_pool(name="quantised", bufs=1))
        per_token_tile = stack.enter_context(tc.tile_pool(name="per_token_tile", bufs=TOKEN_TILES))
        per_chunk = stack.enter_context(tc.tile_pool(name="per_chunk", bufs=2))
        outs = stack.enter_context(tc.tile_pool(name="outs", bufs=3 * TOKEN_TILES))
        turn = stack.enter_context(tc.psum_pool(name="turn", bufs=PSUM_BANKS // 2))
        acc = stack.enter_context(tc.psum_pool(name="acc", bufs=PSUM_BANKS // 2))
        stack.enter_context(tc.manual_schedule())

        small_a = const.tile([P, FACTORS_A], BF16, name="small_a")
        nc.vector.memset(small_a[:], 0.0)
        nc.sync.dma_start(out=small_a[0:1, :], in_=skv_a_lat.rearrange("(o a) b -> o (a b)", o=1))
        small_b = const.tile([P, 2 * FACTORS_B + LATENT], BF16, name="small_b")
        nc.vector.memset(small_b[:], 0.0)
        nc.scalar.dma_start(
            out=small_b[0:1, 0:FACTORS_B], in_=skv_b.rearrange("(o a) b -> o (a b)", o=1)
        )
        nc.scalar.dma_start(
            out=small_b[0:1, 2 * FACTORS_B :], in_=kv_ln_w.rearrange("(o c) -> o c", o=1)
        )
        ones = const.tile([P, P], BF16, name="ones")
        nc.vector.memset(ones[:], 1.0)
        eps = const.tile([P, 1], F32, name="eps")
        nc.vector.memset(eps[:], EPS)
        warm = const.tile([P, 1], F32, name="warm")
        nc.scalar.activation(out=warm[:], in_=eps[:], func=ACT.Sqrt)
        ident = const.tile([P, P], F32, name="ident")
        make_identity(nc, ident[:])

        wa_raw = []
        for r in range(LATENT_TILES):
            rows = loaded.tile([P, HIDDEN], BF16, name="wa_raw%d" % r)
            nc.sync.dma_start(out=rows[:], in_=wkv_a_lat[P * r : P * r + P, :])
            wa_raw.append(rows)
        x_raw = []
        for m in range(TOKEN_TILES):
            rows = loaded.tile([P, HIDDEN], BF16, name="x_raw%d" % m)
            nc.sync.dma_start(out=rows[:], in_=hidden_states[P * m : P * m + P, :])
            x_raw.append(rows)
        chunks = [(kind, group) for kind in range(KINDS) for group in range(CHUNKS_PER_KIND)]
        wb_blocks = wkv_b.rearrange("(h k p) c -> p k h c", k=KINDS, p=P)
        wb_raw = []
        for c, (kind, group) in enumerate(chunks):
            rows = loaded.tile([P, HEADS_PER_CHUNK, LATENT], BF16, name="wb_raw%d" % c)
            head = HEADS_PER_CHUNK * group
            nc.sync.dma_start(out=rows[:], in_=wb_blocks[:, kind, head : head + HEADS_PER_CHUNK, :])
            wb_raw.append(rows)

        def pick_factors(picked, spread, count):
            for q in range(PACK):
                quadrant = slice(QUADRANT * q, QUADRANT * q + QUADRANT)
                nc.vector.tensor_copy(
                    out=picked[quadrant],
                    in_=spread[quadrant]
                    .rearrange("p (x b) -> p x b", b=PACK)[:, :, q : q + 1]
                    .to_broadcast([QUADRANT, count, PACK]),
                )

        sa_k = const.tile([P, LATENT_TILES, PASSES_A, PACK], BF16, name="sa_k")
        sa_ps = acc.tile([P, FACTORS_A], F32, tag="acc")
        nc.tensor.matmul(out=sa_ps[:], lhsT=ones[:], rhs=small_a[:], start=True, stop=True)
        pick_factors(
            sa_k[:].rearrange("p r g t -> p (r g) t"), sa_ps[:], FACTORS_A // PACK
        )

        sb_k = const.tile([P, HEADS, KINDS, PACK], BF16, name="sb_k")
        gain = const.tile([P, LATENT], F32, name="gain")

        def spread_small_b():
            sb_ps = acc.tile([P, 2 * FACTORS_B], F32, tag="acc")
            nc.tensor.matmul(
                out=sb_ps[:], lhsT=ones[:], rhs=small_b[:, 0 : 2 * FACTORS_B], start=True, stop=True
            )
            pick_factors(
                sb_k[:].rearrange("p h k t -> p (h k) t"),
                sb_ps[:, 0:FACTORS_B],
                FACTORS_B // PACK,
            )
            gain_ps = acc.tile([P, LATENT], F32, tag="acc")
            nc.tensor.matmul(
                out=gain_ps[:], lhsT=ones[:], rhs=small_b[:, 2 * FACTORS_B :], start=True, stop=True
            )
            nc.scalar.copy(out=gain[:], in_=gain_ps[:])

        wa_grouped = quantised.tile(
            [P, PASSES_A, LATENT, PACK], BF16, name="wa_grouped", align_bytes=64
        )
        wa_codes = quantised.tile([P, PASSES_A, LATENT], U32, name="wa_codes", align_bytes=64)
        wa_scales = quantised.tile([P, PASSES_A, LATENT], U8, name="wa_scales", align_bytes=64)
        x_codes = quantised.tile([P, TOKEN_TILES, PASSES_A, P], U32, name="x_codes", align_bytes=64)
        x_scales = quantised.tile([P, TOKEN_TILES, PASSES_A, P], U8, name="x_scales", align_bytes=64)
        h_codes = quantised.tile([P, TOKEN_TILES, P], U32, name="h_codes", align_bytes=64)
        h_scales = quantised.tile([P, TOKEN_TILES, P], U8, name="h_scales", align_bytes=64)
        wb_codes = quantised.tile([P, CHUNKS, BANK], U32, name="wb_codes", align_bytes=64)
        wb_scales = quantised.tile([P, CHUNKS, BANK], U8, name="wb_scales", align_bytes=64)

        def turn_four(words, first):
            bank = turn.tile([P, 2, 2, P], F32, tag="turned")
            for i in range(2):
                for u in range(2):
                    nc.tensor.transpose(
                        bank[:, u, i, :], words[:, first + i, u : 2 * P : 2], ident[:]
                    )
            return bank

        def scale_out(bank, factors, grouped):
            nc.vector.tensor_tensor(
                out=grouped.rearrange("p i j (u e) -> p i j u e", e=2),
                in0=bank[:].bitcast(BF16).rearrange("p u i (j e) -> p i j u e", e=2),
                in1=factors.rearrange("p i (u e) -> p i u e", e=2)
                .unsqueeze(2)
                .to_broadcast([P, 2, P, 2, 2]),
                op=ALU.mult,
            )

        def prepare_wa(r):
            words = wa_raw[r][:].bitcast(F32).rearrange("p (g w) -> p g w", g=PASSES_A)
            for g in range(0, PASSES_A, 2):
                bank = turn_four(words, g)
                scale_out(
                    bank, sa_k[:, r, g : g + 2, :], wa_grouped[:, g : g + 2, P * r : P * r + P, :]
                )

        def quantise_wa(g):
            nc.vector.quantize_mx(
                out=wa_codes[:, g, :].bitcast(FP8X4),
                scales=wa_scales[:, g, :],
                in_=wa_grouped[:, g, :, :].rearrange("p o t -> p (o t)"),
            )

        x_grouped = {}

        def turn_x(m):
            words = x_raw[m][:].bitcast(F32).rearrange("p (g w) -> p g w", g=PASSES_A)
            grouped = per_token_tile.tile(
                [P, PASSES_A, P, PACK], BF16, tag="x_grouped", align_bytes=64
            )
            for g in range(0, PASSES_A, 2):
                bank = turn_four(words, g)
                nc.scalar.copy(
                    out=grouped[:].bitcast(F32)[:, g : g + 2, :, :],
                    in_=bank[:].rearrange("p u g j -> p g j u"),
                )
            x_grouped[m] = grouped

        def quantise_x(m):
            nc.vector.quantize_mx(
                out=x_codes[:, m, :, :].rearrange("p g j -> p (g j)").bitcast(FP8X4),
                scales=x_scales[:, m, :, :].rearrange("p g j -> p (g j)"),
                in_=x_grouped[m][:].rearrange("p g j t -> p (g j t)"),
            )

        h_rows = {}

        def latent(m):
            lat = acc.tile([P, LATENT], F32, tag="acc")
            for g in range(PASSES_A):
                nc.tensor.matmul_mx(
                    out=lat[:],
                    lhsT=x_codes[:, m, g, :].bitcast(FP8X4),
                    lhsT_scale=x_scales[:, m, g, :],
                    rhs=wa_codes[:, g, :].bitcast(FP8X4),
                    rhs_scale=wa_scales[:, g, :],
                    start=(g == 0),
                    stop=(g == PASSES_A - 1),
                )
            squares = per_token_tile.tile([P, LATENT], BF16, tag="squares")
            sum_sq = per_token_tile.tile([P, 1], F32, tag="sum_sq")
            nc.scalar.activation(out=squares[:], in_=lat[:], func=ACT.Square, accum_out=sum_sq[:])
            rms = per_token_tile.tile([P, 1], F32, tag="rms")
            nc.scalar.activation(
                out=rms[:], in_=sum_sq[:], func=ACT.Sqrt, scale=1.0 / LATENT, bias=eps[:]
            )
            inv_rms = per_token_tile.tile([P, 1], F32, tag="inv_rms")
            nc.vector.reciprocal(out=inv_rms[:], in_=rms[:])
            h_sb = per_token_tile.tile([P, LATENT], BF16, tag="h_sb")
            nc.vector.scalar_tensor_tensor(
                out=h_sb[:],
                in0=lat[:],
                scalar=inv_rms[:],
                in1=gain[:],
                op0=ALU.mult,
                op1=ALU.mult,
            )
            h_rows[m] = h_sb

        h_grouped = {}

        def turn_h(m):
            words = h_rows[m][:].bitcast(F32)
            bank = acc.tile([P, 2, P], F32, tag="acc")
            for u in range(2):
                nc.tensor.transpose(bank[:, u, :], words[:, u : 2 * P : 2], ident[:])
            grouped = per_token_tile.tile([P, P, PACK], BF16, tag="h_grouped", align_bytes=64)
            nc.scalar.copy(out=grouped[:].bitcast(F32), in_=bank[:].rearrange("p u j -> p j u"))
            h_grouped[m] = grouped

        def quantise_h(m):
            nc.vector.quantize_mx(
                out=h_codes[:, m, :].bitcast(FP8X4),
                scales=h_scales[:, m, :],
                in_=h_grouped[m][:].rearrange("p j t -> p (j t)"),
            )

        wb_banks = {}
        wb_grouped = {}

        def turn_wb(c):
            words = wb_raw[c][:].bitcast(F32)
            wb_banks[c] = [turn_four(words, i) for i in range(0, HEADS_PER_CHUNK, 2)]

        def scale_wb(c):
            kind, group = chunks[c]
            grouped = per_chunk.tile(
                [P, HEADS_PER_CHUNK, P, PACK], BF16, tag="wb_grouped", align_bytes=64
            )
            for b, bank in enumerate(wb_banks[c]):
                head = HEADS_PER_CHUNK * group + 2 * b
                scale_out(
                    bank, sb_k[:, head : head + 2, kind, :], grouped[:, 2 * b : 2 * b + 2, :, :]
                )
            wb_grouped[c] = grouped

        def quantise_wb(c):
            nc.vector.quantize_mx(
                out=wb_codes[:, c, :].bitcast(FP8X4),
                scales=wb_scales[:, c, :],
                in_=wb_grouped[c][:].rearrange("p i j t -> p (i j t)"),
            )

        kv_banks = {}

        def project(c):
            for m in range(TOKEN_TILES):
                kv = acc.tile([P, BANK], F32, tag="acc")
                nc.tensor.matmul_mx(
                    out=kv[:],
                    lhsT=h_codes[:, m, :].bitcast(FP8X4),
                    lhsT_scale=h_scales[:, m, :],
                    rhs=wb_codes[:, c, :].bitcast(FP8X4),
                    rhs_scale=wb_scales[:, c, :],
                    start=True,
                    stop=True,
                )
                kv_banks[m] = kv

        def store(c):
            kind, group = chunks[c]
            head = HEADS_PER_CHUNK * group
            for m in range(TOKEN_TILES):
                out_sb = outs.tile([P, BANK], F32, tag="out_sb")
                nc.scalar.copy(out=out_sb[:], in_=kv_banks[m][:])
                nc.sync.dma_start(
                    out=(out_0, out_1)[kind][
                        P * m : P * m + P, head : head + HEADS_PER_CHUNK, :
                    ].rearrange("p h d -> p (h d)"),
                    in_=out_sb[:],
                )

        for r in range(LATENT_TILES):
            prepare_wa(r)
        turn_x(0)
        turn_x(1)
        for g in range(PASSES_A):
            quantise_wa(g)
        for m in range(TOKEN_TILES):
            quantise_x(m)
            if m + 2 < TOKEN_TILES:
                turn_x(m + 2)
        spread_small_b()
        for m in range(TOKEN_TILES):
            latent(m)
        turn_wb(0)
        turn_wb(1)
        for m in range(TOKEN_TILES):
            turn_h(m)
        scale_wb(0)
        quantise_h(0)
        quantise_h(1)
        quantise_wb(0)
        quantise_h(2)
        quantise_h(3)
        scale_wb(1)
        for c in range(CHUNKS):
            project(c)
            if c + 2 < CHUNKS:
                turn_wb(c + 2)
            if c + 1 < CHUNKS:
                quantise_wb(c + 1)
            store(c)
            if c + 2 < CHUNKS:
                scale_wb(c + 2)
